import numpy as np
import ml_dtypes


def mxq(x, axis, fmt="e4m3"):
    dtype, down = {"e4m3": (ml_dtypes.float8_e4m3fn, 7), "e5m2": (ml_dtypes.float8_e5m2, 14)}[fmt]
    v = np.moveaxis(np.asarray(x, np.float32).astype(ml_dtypes.bfloat16).astype(np.float64), axis, -1)
    blocks = v.reshape(v.shape[:-1] + (-1, 32))
    amax = np.abs(blocks).max(-1, keepdims=True)
    byte = np.maximum(np.where(amax > 0, np.frexp(amax)[1] - 1 + 127, 0) - down, 1)
    scale = np.exp2(byte - 127.0)
    codes = (blocks / scale).astype(np.float32).astype(dtype).astype(np.float64)
    return np.moveaxis((codes * scale).reshape(v.shape), -1, axis)


WIDE = False


def mx_kscale(k):
    if not WIDE:
        return np.ones(k)
    levels = np.array([10, -10, 5, -5, 0])
    if k % 512:
        return np.exp2(np.random.permutation(np.resize(levels, k // 32))).repeat(32)
    a = np.empty((k // 512, 16))
    for p in range(k // 512):
        a[p, :8] = np.random.permutation(np.resize(levels, 8))
        for g in range(8):
            far = levels[np.abs(levels - a[p, g]) >= 10]
            a[p, g + 8] = far[np.random.randint(len(far))]
    return np.exp2(a.ravel()).repeat(32)


BF16 = ml_dtypes.bfloat16


def bf(x):
    return np.asarray(x, np.float32).astype(BF16)


def f64(x):
    return np.asarray(x).astype(np.float64)


B, SEQ, FEAT, OUT, H1, H2 = 4096, 16, 16, 512, 512, 512
D = SEQ * FEAT


def setup_inputs():
    s, t = mx_kscale(H1), mx_kscale(H2)
    return {"h1": bf(np.random.standard_normal((B, H1))),
            "h2": bf(np.random.standard_normal((B, H2)) * 0.7),
            "W1": bf(np.random.standard_normal((H1, D)) / np.sqrt(D) * s[:, None]),
            "W2": bf(np.random.standard_normal((H2, H1)) / np.sqrt(H1) * t[:, None] / s[None, :]),
            "W3": bf(np.random.standard_normal((D, H2)) / np.sqrt(H2) / t[None, :])}


def reference(h1, h2, W1, W2, W3):
    h1, h2, W1, W2, W3 = f64(h1), f64(h2), f64(W1), f64(W2), f64(W3)
    m1 = np.where(h1 > 0, 1.0, 0.0)
    m2 = np.where(h2 > 0, 1.0, 0.0)
    w1_rows = W1.sum(axis=1)
    a = (mxq(m1 * w1_rows, 1, "e4m3") @ mxq(W2, 1, "e4m3").T) * m2
    row = mxq(a, 1, "e4m3") @ mxq(W3, 1, "e4m3").T
    w3_cols = W3.sum(axis=0)
    c = (mxq(m2 * w3_cols, 1, "e4m3") @ mxq(W2, 0, "e4m3")) * m1
    col = mxq(c, 1, "e4m3") @ mxq(W1, 0, "e4m3")
    return row - col

@@ -1,0 +1,298 @@
+from contextlib import ExitStack
+
+import concourse.mybir as mybir
+from concourse.masks import make_identity
+
+FLOPS = 2 * 4096 * 512 * 512 * 2 + 2 * 4096 * 512 * 256 * 2
+
+FP8X4 = mybir.dt.float8_e4m3fn_x4
+BF16 = mybir.dt.bfloat16
+F32 = mybir.dt.float32
+U32 = mybir.dt.uint32
+U8 = mybir.dt.uint8
+ALU = mybir.AluOpType
+ACT = mybir.ActivationFunctionType
+AX = mybir.AxisListType
+
+P = 128
+B = 4096
+H = 512
+D = 256
+NCH = B // P
+NB = 2
+SIZES = [2] * 15 + [1, 1]
+GROUPS = [2, 2, 4, 4, 4, 4, 4, 4, 4]
+LT = 1
+LM = 1
+LA = 3
+LO = 1
+PIN = True
+
+
+def tile_divergencefreemlp_pa_t_kernel(tc, h1, h2, W1, W2, W3, out):
+    nc = tc.nc
+    NR = len(SIZES)
+    starts = [sum(SIZES[:k]) for k in range(NR)]
+    with ExitStack() as ctx:
+        const = ctx.enter_context(tc.tile_pool(name="const", bufs=1))
+        work = ctx.enter_context(tc.tile_pool(name="work", bufs=3))
+        psum_ht = ctx.enter_context(tc.psum_pool(name="psum_ht", bufs=2))
+        psum_ac = ctx.enter_context(tc.psum_pool(name="psum_ac", bufs=4))
+        psum_o = ctx.enter_context(tc.psum_pool(name="psum_o", bufs=2))
+        if PIN:
+            ctx.enter_context(tc.manual_schedule())
+
+        raw1 = const.tile([P, 4 * D], BF16, name="raw1")
+        raw3 = const.tile([P, 2 * H], BF16, name="raw3")
+        raw2 = const.tile([P, 4 * H], BF16, name="raw2")
+        nc.sync.dma_start(
+            out=raw3[:].rearrange("p (t i) -> p t i", t=2),
+            in_=W3.rearrange("(t p) i -> p t i", p=P),
+        )
+        nc.sync.dma_start(
+            out=raw1[:],
+            in_=W1.rearrange("(p t) d -> p (t d)", t=4),
+        )
+        hv = [h1.rearrange("(p n) j -> p n j", n=NCH), h2.rearrange("(p n) j -> p n j", n=NCH)]
+        where = {}
+        n0 = 0
+        for g, ln in enumerate(GROUPS):
+            for x in range(2):
+                hs = const.tile([P, ln * H], BF16, name="h%d_%d" % (x, g))
+                nc.sync.dma_start(
+                    out=hs[:].rearrange("p (n j) -> p n j", n=ln), in_=hv[x][:, n0 : n0 + ln, :]
+                )
+                for l in range(ln):
+                    where[(x, n0 + l)] = (hs, l)
+            n0 += ln
+            if g == 0:
+                nc.sync.dma_start(
+                    out=raw2[:],
+                    in_=W2.rearrange("(p t) j -> p (t j)", t=4),
+                )
+        outv = out.rearrange("(p n) d -> p n d", n=NCH)
+
+        ident = const.tile([P, P], F32, name="ident")
+        make_identity(nc, ident[:])
+        gw = const.tile([P, 6144], BF16, name="gw", align_bytes=64)
+        gww = gw[:].bitcast(F32)
+        wcodes = const.tile([P, 1536], U32, name="wcodes", align_bytes=64)
+        wscales = const.tile([P, 1536], U8, name="wscales", align_bytes=64)
+        wsum = const.tile([P, 8], F32, name="wsum")
+        wc = const.tile([P, 2 * NB * H], BF16, name="wc")
+
+        nc.gpsimd.tensor_scalar(
+            out=gw[:, 5120:6144].rearrange("p (d t) -> p d t", t=4),
+            in0=raw1[:].rearrange("p (t d) -> p d t", t=4),
+            scalar1=-1.0,
+            scalar2=0.0,
+            op0=ALU.mult,
+            op1=ALU.add,
+        )
+        nc.vector.tensor_reduce(
+            out=wsum[:, 0:4], in_=raw1[:].rearrange("p (t d) -> p t d", t=4), axis=AX.X, op=ALU.add
+        )
+        raw3w = raw3[:].bitcast(F32)
+        ps3 = psum_ht.tile([P, 512], F32, name="ps3", tag="ht")
+        for dh in range(2):
+            for u in range(2):
+                nc.tensor.transpose(
+                    out=ps3[:, u * 256 + dh * P : u * 256 + (dh + 1) * P],
+                    in_=raw3w[:, dh * 256 + u : (dh + 1) * 256 : 2],
+                    identity=ident[:],
+                )
+        nc.scalar.copy(
+            out=gww[:, 2048:2560].rearrange("p (c u) -> p c u", u=2),
+            in_=ps3[:].rearrange("p (u c) -> p c u", u=2),
+        )
+        nc.vector.tensor_reduce(
+            out=wsum[:, 4:8], in_=gw[:, 4096:5120].rearrange("p (d t) -> p t d", t=4), axis=AX.X, op=ALU.add
+        )
+        nc.vector.tensor_copy(
+            out=wc[:].rearrange("p (x c b t) -> p x c b t", x=2, c=NB, t=4)[:, :, 0, :, :],
+            in_=wsum[:].rearrange("p (x t) -> p x t", x=2).unsqueeze(2).to_broadcast([P, 2, P, 4]),
+        )
+        wcv = wc[:].rearrange("p (x c w) -> p x c w", x=2, c=NB)
+        nc.vector.tensor_copy(out=wcv[:, :, 1, :], in_=wcv[:, :, 0, :])
+
+        hts = {}
+        mtiles = {}
+        ups = {}
+        upcodes = {}
+        acbs = {}
+        acms = {}
+        accodes = {}
+
+        def transposes(k):
+            nb = SIZES[k]
+            ht_sb = work.tile([P, 2 * nb * H], BF16, name="ht_sb", tag="ht_sb", bufs=LT + 2)
+            htw = ht_sb[:].bitcast(F32).rearrange("p (x c w) -> p x c w", x=2, c=nb)
+            banks = []
+            for c in range(nb):
+                bank = psum_ht.tile([P, 512], F32, name="ht", tag="ht")
+                for x in range(2):
+                    src, l = where[(x, starts[k] + c)]
+                    srcw = src[:].bitcast(F32)
+                    for u in range(2):
+                        nc.tensor.transpose(
+                            out=bank[:, (2 * x + u) * P : (2 * x + u + 1) * P],
+                            in_=srcw[:, l * 256 + u : (l + 1) * 256 : 2],
+                            identity=ident[:],
+                        )
+                banks.append(bank)
+            for c in range(nb):
+                nc.scalar.copy(
+                    out=htw[:, :, c, :].rearrange("p x (b u) -> p x b u", u=2),
+                    in_=banks[c][:].rearrange("p (x u b) -> p x b u", x=2, u=2),
+                )
+            hts[k] = ht_sb
+
+        def make_mask(k):
+            m = work.tile([P, 2 * SIZES[k] * H], BF16, name="mask", tag="mask", bufs=LA + LM + 2)
+            nc.vector.tensor_single_scalar(out=m[:], in_=hts[k][:], scalar=0.0, op=ALU.is_gt)
+            mtiles[k] = m
+
+        def make_up(k):
+            nb = SIZES[k]
+            up = work.tile([P, 2 * nb * H], BF16, name="up", tag="up", bufs=2, align_bytes=64)
+            nc.vector.tensor_tensor(
+                out=up[:].rearrange("p (x c w) -> p x c w", x=2, c=nb),
+                in0=mtiles[k][:].rearrange("p (x c w) -> p x c w", x=2, c=nb),
+                in1=wcv[:, :, 0:nb, :],
+                op=ALU.mult,
+            )
+            ups[k] = up
+
+        def quantise(src, nb, tag):
+            codes = work.tile([P, 2 * nb * P], U32, name=tag + "_c", tag=tag + "_c", bufs=3, align_bytes=64)
+            scales = work.tile([P, 2 * nb * P], U8, name=tag + "_s", tag=tag + "_s", bufs=3, align_bytes=64)
+            nc.vector.quantize_mx(out=codes[:].bitcast(FP8X4), scales=scales[:], in_=src[:])
+            return (codes, scales)
+
+        def first_matmuls(k):
+            nb = SIZES[k]
+            codes, scales = upcodes[k]
+            acb = work.tile([P, 2 * nb * H], BF16, name="acb", tag="acb", bufs=LA + 1)
+            for c in range(nb):
+                for xin in range(2):
+                    xo = 1 - xin
+                    ps = psum_ac.tile([P, 512], F32, name="ac", tag="ac")
+                    lo = xin * nb * P + c * P
+                    for t in range(4):
+                        wlo = 512 * xin + t * P
+                        nc.tensor.matmul_mx(
+                            out=ps[:, t * P : (t + 1) * P],
+                            lhsT=wcodes[:, wlo : wlo + P].bitcast(FP8X4),
+                            lhsT_scale=wscales[:, wlo : wlo + P],
+                            rhs=codes[:, lo : lo + P].bitcast(FP8X4),
+                            rhs_scale=scales[:, lo : lo + P],
+                            start=True,
+                            stop=True,
+                        )
+                    olo = xo * nb * H + c * H
+                    nc.scalar.copy(
+                        out=acb[:, olo : olo + H].rearrange("p (b t) -> p b t", t=4),
+                        in_=ps[:].rearrange("p (t b) -> p b t", t=4),
+                    )
+            acbs[k] = acb
+
+        def mask_ac(k):
+            acm = work.tile([P, 2 * SIZES[k] * H], BF16, name="acm", tag="acm", bufs=2, align_bytes=64)
+            nc.vector.tensor_tensor(out=acm[:], in0=acbs[k][:], in1=mtiles[k][:], op=ALU.mult)
+            acms[k] = acm
+
+        def last_matmuls(k):
+            nb = SIZES[k]
+            codes, scales = accodes[k]
+            o = psum_o.tile([P, nb * D], F32, name="o", tag="o")
+            for c in range(nb):
+                alo = nb * P + c * P
+                clo = c * P
+                nc.tensor.matmul_mx(
+                    out=o[:, c * D : (c + 1) * D],
+                    lhsT=codes[:, alo : alo + P].bitcast(FP8X4),
+                    lhsT_scale=scales[:, alo : alo + P],
+                    rhs=wcodes[:, 1024:1280].bitcast(FP8X4),
+                    rhs_scale=wscales[:, 1024:1280],
+                    start=True,
+                    stop=False,
+                )
+                nc.tensor.matmul_mx(
+                    out=o[:, c * D : (c + 1) * D],
+                    lhsT=codes[:, clo : clo + P].bitcast(FP8X4),
+                    lhsT_scale=scales[:, clo : clo + P],
+                    rhs=wcodes[:, 1280:1536].bitcast(FP8X4),
+                    rhs_scale=wscales[:, 1280:1536],
+                    start=False,
+                    stop=True,
+                )
+            osb = work.tile([P, nb * D], F32, name="osb", tag="osb", bufs=3)
+            nc.scalar.copy(out=osb[:], in_=o[:])
+            nc.sync.dma_start(
+                out=outv[:, starts[k] : starts[k] + nb, :], in_=osb[:].rearrange("p (n d) -> p n d", n=nb)
+            )
+
+        def quantise_weights(s):
+            nc.vector.quantize_mx(
+                out=wcodes[:, s * 512 : (s + 1) * 512].bitcast(FP8X4),
+                scales=wscales[:, s * 512 : (s + 1) * 512],
+                in_=gw[:, s * 2048 : (s + 1) * 2048],
+            )
+
+        transposes(0)
+        make_mask(0)
+
+        raw2w = raw2[:].bitcast(F32)
+        for g in range(2):
+            ps2 = psum_ht.tile([P, 512], F32, name="ps2", tag="ht")
+            for tt in range(2):
+                t = 2 * g + tt
+                for u in range(2):
+                    nc.tensor.transpose(
+                        out=ps2[:, u * 256 + tt * P : u * 256 + (tt + 1) * P],
+                        in_=raw2w[:, t * 256 + u : (t + 1) * 256 : 2],
+                        identity=ident[:],
+                    )
+            nc.scalar.copy(
+                out=gww[:, g * 512 : (g + 1) * 512].rearrange("p (c u) -> p c u", u=2),
+                in_=ps2[:].rearrange("p (u c) -> p c u", u=2),
+            )
+        raw2v = raw2[:].rearrange("p (t q s) -> p t q s", t=4, q=P, s=4)
+        for s in range(4):
+            lo = 2048 + s * H
+            nc.gpsimd.tensor_scalar(
+                out=gw[:, lo : lo + H].rearrange("p (q t) -> p q t", t=4),
+                in0=raw2v[:, :, :, s].rearrange("p t q -> p q t"),
+                scalar1=1.0,
+                scalar2=0.0,
+                op0=ALU.mult,
+                op1=ALU.add,
+            )
+        for k in range(1, LM + LT):
+            transposes(k)
+        for k in range(1, LM):
+            make_mask(k)
+
+        for i in range(NR + LA + LO):
+            if 0 <= i - 1 < NR:
+                first_matmuls(i - 1)
+            if 0 <= i - LA - LO < NR:
+                last_matmuls(i - LA - LO)
+            if i + LM + LT < NR:
+                transposes(i + LM + LT)
+            if 0 <= i - LA < NR:
+                mask_ac(i - LA)
+            if i < NR:
+                make_up(i)
+            if i == 0:
+                quantise_weights(0)
+            if 0 <= i - LA < NR:
+                accodes[i - LA] = quantise(acms[i - LA], SIZES[i - LA], "ac")
+            if i < NR:
+                upcodes[i] = quantise(ups[i], SIZES[i], "up")
+            if i == 0:
+                quantise_weights(1)
+            if i + LM < NR:
+                make_mask(i + LM)
+            if i == 0:
+                quantise_weights(2)

@@ -19,218 +19,165 @@ B = 4096
 H = 512
 D = 256
 NCH = B // P
-NB = 2
-SIZES = [2] * 15 + [1, 1]
-GROUPS = [2, 2, 4, 4, 4, 4, 4, 4, 4]
-LT = 1
-LM = 1
-LA = 3
-LO = 1
-PIN = True
+GROUPS = [1, 1, 2, 4, 4, 4, 4, 4, 4, 4]
+L = 3
 
 
 def tile_divergencefreemlp_pa_t_kernel(tc, h1, h2, W1, W2, W3, out):
     nc = tc.nc
-    NR = len(SIZES)
-    starts = [sum(SIZES[:k]) for k in range(NR)]
     with ExitStack() as ctx:
         const = ctx.enter_context(tc.tile_pool(name="const", bufs=1))
         work = ctx.enter_context(tc.tile_pool(name="work", bufs=3))
-        psum_ht = ctx.enter_context(tc.psum_pool(name="psum_ht", bufs=2))
-        psum_ac = ctx.enter_context(tc.psum_pool(name="psum_ac", bufs=4))
-        psum_o = ctx.enter_context(tc.psum_pool(name="psum_o", bufs=2))
-        if PIN:
-            ctx.enter_context(tc.manual_schedule())
+        psum_m = ctx.enter_context(tc.psum_pool(name="psum_m", bufs=5))
+        psum_ac = ctx.enter_context(tc.psum_pool(name="psum_ac", bufs=2))
+        psum_o = ctx.enter_context(tc.psum_pool(name="psum_o", bufs=1))
+        ctx.enter_context(tc.manual_schedule())
 
         raw1 = const.tile([P, 4 * D], BF16, name="raw1")
         raw3 = const.tile([P, 2 * H], BF16, name="raw3")
         raw2 = const.tile([P, 4 * H], BF16, name="raw2")
-        nc.sync.dma_start(
-            out=raw3[:].rearrange("p (t i) -> p t i", t=2),
-            in_=W3.rearrange("(t p) i -> p t i", p=P),
-        )
-        nc.sync.dma_start(
-            out=raw1[:],
-            in_=W1.rearrange("(p t) d -> p (t d)", t=4),
-        )
         hv = [h1.rearrange("(p n) j -> p n j", n=NCH), h2.rearrange("(p n) j -> p n j", n=NCH)]
         where = {}
         n0 = 0
         for g, ln in enumerate(GROUPS):
+            hs = const.tile([P, 2 * ln * H], BF16, name="h_%d" % g)
             for x in range(2):
-                hs = const.tile([P, ln * H], BF16, name="h%d_%d" % (x, g))
                 nc.sync.dma_start(
-                    out=hs[:].rearrange("p (n j) -> p n j", n=ln), in_=hv[x][:, n0 : n0 + ln, :]
+                    out=hs[:, x * ln * H : (x + 1) * ln * H].rearrange("p (n j) -> p n j", n=ln),
+                    in_=hv[x][:, n0 : n0 + ln, :],
                 )
-                for l in range(ln):
-                    where[(x, n0 + l)] = (hs, l)
+            for l in range(ln):
+                where[n0 + l] = (hs, ln, l)
             n0 += ln
             if g == 0:
                 nc.sync.dma_start(
-                    out=raw2[:],
-                    in_=W2.rearrange("(p t) j -> p (t j)", t=4),
+                    out=raw3[:].rearrange("p (t i) -> p t i", t=2),
+                    in_=W3.rearrange("(t p) i -> p t i", p=P),
                 )
+                nc.sync.dma_start(out=raw1[:], in_=W1.rearrange("(p t) d -> p (t d)", t=4))
+                nc.sync.dma_start(out=raw2[:], in_=W2.rearrange("(p t) j -> p (t j)", t=4))
         outv = out.rearrange("(p n) d -> p n d", n=NCH)
 
         ident = const.tile([P, P], F32, name="ident")
         make_identity(nc, ident[:])
+        ones = const.tile([P, 1], BF16, name="ones")
+        nc.vector.memset(ones[:], 1.0)
         gw = const.tile([P, 6144], BF16, name="gw", align_bytes=64)
         gww = gw[:].bitcast(F32)
         wcodes = const.tile([P, 1536], U32, name="wcodes", align_bytes=64)
         wscales = const.tile([P, 1536], U8, name="wscales", align_bytes=64)
         wsum = const.tile([P, 8], F32, name="wsum")
-        wc = const.tile([P, 2 * NB * H], BF16, name="wc")
+        wb = const.tile([P, 8], BF16, name="wb")
+        junk = const.tile([P, D], BF16, name="junk")
 
-        nc.gpsimd.tensor_scalar(
-            out=gw[:, 5120:6144].rearrange("p (d t) -> p d t", t=4),
-            in0=raw1[:].rearrange("p (t d) -> p d t", t=4),
-            scalar1=-1.0,
-            scalar2=0.0,
-            op0=ALU.mult,
-            op1=ALU.add,
-        )
-        nc.vector.tensor_reduce(
-            out=wsum[:, 0:4], in_=raw1[:].rearrange("p (t d) -> p t d", t=4), axis=AX.X, op=ALU.add
-        )
-        raw3w = raw3[:].bitcast(F32)
-        ps3 = psum_ht.tile([P, 512], F32, name="ps3", tag="ht")
-        for dh in range(2):
-            for u in range(2):
-                nc.tensor.transpose(
-                    out=ps3[:, u * 256 + dh * P : u * 256 + (dh + 1) * P],
-                    in_=raw3w[:, dh * 256 + u : (dh + 1) * 256 : 2],
-                    identity=ident[:],
-                )
-        nc.scalar.copy(
-            out=gww[:, 2048:2560].rearrange("p (c u) -> p c u", u=2),
-            in_=ps3[:].rearrange("p (u c) -> p c u", u=2),
-        )
-        nc.vector.tensor_reduce(
-            out=wsum[:, 4:8], in_=gw[:, 4096:5120].rearrange("p (d t) -> p t d", t=4), axis=AX.X, op=ALU.add
-        )
-        nc.vector.tensor_copy(
-            out=wc[:].rearrange("p (x c b t) -> p x c b t", x=2, c=NB, t=4)[:, :, 0, :, :],
-            in_=wsum[:].rearrange("p (x t) -> p x t", x=2).unsqueeze(2).to_broadcast([P, 2, P, 4]),
-        )
-        wcv = wc[:].rearrange("p (x c w) -> p x c w", x=2, c=NB)
-        nc.vector.tensor_copy(out=wcv[:, :, 1, :], in_=wcv[:, :, 0, :])
-
-        hts = {}
+        mnat = {}
         mtiles = {}
-        ups = {}
-        upcodes = {}
+        pairs = {}
+        codes = {}
         acbs = {}
-        acms = {}
-        accodes = {}
-
-        def transposes(k):
-            nb = SIZES[k]
-            ht_sb = work.tile([P, 2 * nb * H], BF16, name="ht_sb", tag="ht_sb", bufs=LT + 2)
-            htw = ht_sb[:].bitcast(F32).rearrange("p (x c w) -> p x c w", x=2, c=nb)
-            banks = []
-            for c in range(nb):
-                bank = psum_ht.tile([P, 512], F32, name="ht", tag="ht")
-                for x in range(2):
-                    src, l = where[(x, starts[k] + c)]
-                    srcw = src[:].bitcast(F32)
-                    for u in range(2):
-                        nc.tensor.transpose(
-                            out=bank[:, (2 * x + u) * P : (2 * x + u + 1) * P],
-                            in_=srcw[:, l * 256 + u : (l + 1) * 256 : 2],
-                            identity=ident[:],
-                        )
-                banks.append(bank)
-            for c in range(nb):
-                nc.scalar.copy(
-                    out=htw[:, :, c, :].rearrange("p x (b u) -> p x b u", u=2),
-                    in_=banks[c][:].rearrange("p (x u b) -> p x b u", x=2, u=2),
-                )
-            hts[k] = ht_sb
 
         def make_mask(k):
-            m = work.tile([P, 2 * SIZES[k] * H], BF16, name="mask", tag="mask", bufs=LA + LM + 2)
-            nc.vector.tensor_single_scalar(out=m[:], in_=hts[k][:], scalar=0.0, op=ALU.is_gt)
-            mtiles[k] = m
+            hs, ln, l = where[k]
+            hc = hs[:].rearrange("p (x n j) -> p x n j", x=2, n=ln)[:, :, l, :]
+            m = work.tile([P, 2 * H], BF16, name="mask", tag="mask", bufs=4)
+            nc.vector.tensor_single_scalar(
+                out=m[:].rearrange("p (x j) -> p x j", x=2), in_=hc, scalar=0.0, op=ALU.is_gt
+            )
+            mnat[k] = m
+
+        def transposes(k):
+            w = mnat[k][:].bitcast(F32)
+            bank = psum_m.tile([P, 512], F32, name="m", tag="m")
+            for x in range(2):
+                lo = x * 256
+                for u in range(2):
+                    nc.tensor.transpose(
+                        out=bank[:, (2 * u + x) * P : (2 * u + x + 1) * P],
+                        in_=w[:, lo + u : lo + 256 : 2],
+                        identity=ident[:],
+                    )
+            mtiles[k] = bank[:].bitcast(BF16).rearrange("p (u x b e) -> p x b u e", u=2, x=2, e=2)
+
+        def pair(k):
+            if k not in pairs:
+                pairs[k] = work.tile([P, 4 * H], BF16, name="pair", tag="pair", bufs=3, align_bytes=64)
+            return pairs[k]
 
         def make_up(k):
-            nb = SIZES[k]
-            up = work.tile([P, 2 * nb * H], BF16, name="up", tag="up", bufs=2, align_bytes=64)
             nc.vector.tensor_tensor(
-                out=up[:].rearrange("p (x c w) -> p x c w", x=2, c=nb),
-                in0=mtiles[k][:].rearrange("p (x c w) -> p x c w", x=2, c=nb),
-                in1=wcv[:, :, 0:nb, :],
+                out=pair(k)[:, 0 : 2 * H].rearrange("p (x b u e) -> p x b u e", x=2, u=2, e=2),
+                in0=mtiles[k],
+                in1=wb[:].rearrange("p (x u e) -> p x u e", x=2, u=2).unsqueeze(2).to_broadcast([P, 2, P, 2, 2]),
                 op=ALU.mult,
             )
-            ups[k] = up
-
-        def quantise(src, nb, tag):
-            codes = work.tile([P, 2 * nb * P], U32, name=tag + "_c", tag=tag + "_c", bufs=3, align_bytes=64)
-            scales = work.tile([P, 2 * nb * P], U8, name=tag + "_s", tag=tag + "_s", bufs=3, align_bytes=64)
-            nc.vector.quantize_mx(out=codes[:].bitcast(FP8X4), scales=scales[:], in_=src[:])
-            return (codes, scales)
-
-        def first_matmuls(k):
-            nb = SIZES[k]
-            codes, scales = upcodes[k]
-            acb = work.tile([P, 2 * nb * H], BF16, name="acb", tag="acb", bufs=LA + 1)
-            for c in range(nb):
-                for xin in range(2):
-                    xo = 1 - xin
-                    ps = psum_ac.tile([P, 512], F32, name="ac", tag="ac")
-                    lo = xin * nb * P + c * P
-                    for t in range(4):
-                        wlo = 512 * xin + t * P
-                        nc.tensor.matmul_mx(
-                            out=ps[:, t * P : (t + 1) * P],
-                            lhsT=wcodes[:, wlo : wlo + P].bitcast(FP8X4),
-                            lhsT_scale=wscales[:, wlo : wlo + P],
-                            rhs=codes[:, lo : lo + P].bitcast(FP8X4),
-                            rhs_scale=scales[:, lo : lo + P],
-                            start=True,
-                            stop=True,
-                        )
-                    olo = xo * nb * H + c * H
-                    nc.scalar.copy(
-                        out=acb[:, olo : olo + H].rearrange("p (b t) -> p b t", t=4),
-                        in_=ps[:].rearrange("p (t b) -> p b t", t=4),
-                    )
-            acbs[k] = acb
 
         def mask_ac(k):
-            acm = work.tile([P, 2 * SIZES[k] * H], BF16, name="acm", tag="acm", bufs=2, align_bytes=64)
-            nc.vector.tensor_tensor(out=acm[:], in0=acbs[k][:], in1=mtiles[k][:], op=ALU.mult)
-            acms[k] = acm
+            nc.vector.tensor_tensor(
+                out=pair(k + L)[:, 2 * H : 4 * H].rearrange("p (x b u e) -> p x b u e", x=2, u=2, e=2),
+                in0=mtiles[k],
+                in1=acbs[k][:].rearrange("p (x b u e) -> p x b u e", x=2, u=2, e=2),
+                op=ALU.mult,
+            )
+
+        def quantise(k):
+            cd = work.tile([P, 4 * P], U32, name="cd", tag="cd", bufs=3, align_bytes=64)
+            sc = work.tile([P, 4 * P], U8, name="sc", tag="sc", bufs=3, align_bytes=64)
+            lo = 0 if k < NCH else 2
+            hi = 4 if k >= L else 2
+            nc.vector.quantize_mx(
+                out=cd[:, lo * P : hi * P].bitcast(FP8X4),
+                scales=sc[:, lo * P : hi * P],
+                in_=pair(k)[:, lo * H : hi * H],
+            )
+            codes[k] = (cd, sc)
+
+        def first_matmuls(k):
+            cd, sc = codes[k]
+            acb = work.tile([P, 2 * H], BF16, name="acb", tag="acb", bufs=3)
+            for xin in range(2):
+                xo = 1 - xin
+                ps = psum_ac.tile([P, 512], F32, name="ac", tag="ac")
+                for t in range(4):
+                    wlo = 512 * xin + t * P
+                    nc.tensor.matmul_mx(
+                        out=ps[:, t * P : (t + 1) * P],
+                        lhsT=wcodes[:, wlo : wlo + P].bitcast(FP8X4),
+                        lhsT_scale=wscales[:, wlo : wlo + P],
+                        rhs=cd[:, xin * P : (xin + 1) * P].bitcast(FP8X4),
+                        rhs_scale=sc[:, xin * P : (xin + 1) * P],
+                        start=True,
+                        stop=True,
+                    )
+                nc.scalar.copy(
+                    out=acb[:, xo * H : (xo + 1) * H].rearrange("p (b t) -> p b t", t=4),
+                    in_=ps[:].rearrange("p (t b) -> p b t", t=4),
+                )
+            acbs[k] = acb
 
         def last_matmuls(k):
-            nb = SIZES[k]
-            codes, scales = accodes[k]
-            o = psum_o.tile([P, nb * D], F32, name="o", tag="o")
-            for c in range(nb):
-                alo = nb * P + c * P
-                clo = c * P
-                nc.tensor.matmul_mx(
-                    out=o[:, c * D : (c + 1) * D],
-                    lhsT=codes[:, alo : alo + P].bitcast(FP8X4),
-                    lhsT_scale=scales[:, alo : alo + P],
-                    rhs=wcodes[:, 1024:1280].bitcast(FP8X4),
-                    rhs_scale=wscales[:, 1024:1280],
-                    start=True,
-                    stop=False,
-                )
-                nc.tensor.matmul_mx(
-                    out=o[:, c * D : (c + 1) * D],
-                    lhsT=codes[:, clo : clo + P].bitcast(FP8X4),
-                    lhsT_scale=scales[:, clo : clo + P],
-                    rhs=wcodes[:, 1280:1536].bitcast(FP8X4),
-                    rhs_scale=wscales[:, 1280:1536],
-                    start=False,
-                    stop=True,
-                )
-            osb = work.tile([P, nb * D], F32, name="osb", tag="osb", bufs=3)
-            nc.scalar.copy(out=osb[:], in_=o[:])
-            nc.sync.dma_start(
-                out=outv[:, starts[k] : starts[k] + nb, :], in_=osb[:].rearrange("p (n d) -> p n d", n=nb)
+            cd, sc = codes[k + L]
+            o = psum_o.tile([P, D], F32, name="o", tag="o")
+            nc.tensor.matmul_mx(
+                out=o[:],
+                lhsT=cd[:, 3 * P : 4 * P].bitcast(FP8X4),
+                lhsT_scale=sc[:, 3 * P : 4 * P],
+                rhs=wcodes[:, 1024:1280].bitcast(FP8X4),
+                rhs_scale=wscales[:, 1024:1280],
+                start=True,
+                stop=False,
             )
+            nc.tensor.matmul_mx(
+                out=o[:],
+                lhsT=cd[:, 2 * P : 3 * P].bitcast(FP8X4),
+                lhsT_scale=sc[:, 2 * P : 3 * P],
+                rhs=wcodes[:, 1280:1536].bitcast(FP8X4),
+                rhs_scale=wscales[:, 1280:1536],
+                start=False,
+                stop=True,
+            )
+            osb = work.tile([P, D], F32, name="osb", tag="osb", bufs=4)
+            nc.scalar.copy(out=osb[:], in_=o[:])
+            nc.sync.dma_start(out=outv[:, k, :], in_=osb[:])
 
         def quantise_weights(s):
             nc.vector.quantize_mx(
@@ -239,12 +186,40 @@ def tile_divergencefreemlp_pa_t_kernel(tc, h1, h2, W1, W2, W3, out):
                 in_=gw[:, s * 2048 : (s + 1) * 2048],
             )
 
-        transposes(0)
         make_mask(0)
+        pw = psum_o.tile([P, D], F32, name="pw", tag="o")
+        for t in range(4):
+            for dh in range(2):
+                nc.tensor.matmul(
+                    out=pw[:, t : t + 1],
+                    lhsT=raw3[:, dh * H + t : (dh + 1) * H : 4],
+                    rhs=ones[:],
+                    start=dh == 0,
+                    stop=dh == 1,
+                )
+        nc.scalar.copy(out=wsum[:, 4:8], in_=pw[:, 0:4])
+        raw3w = raw3[:].bitcast(F32)
+        ps3 = psum_m.tile([P, 512], F32, name="ps3", tag="m")
+        transposes(0)
+        for dh in range(2):
+            for u in range(2):
+                nc.tensor.transpose(
+                    out=ps3[:, u * 256 + dh * P : u * 256 + (dh + 1) * P],
+                    in_=raw3w[:, dh * 256 + u : (dh + 1) * 256 : 2],
+                    identity=ident[:],
+                )
+        for t in range(2, 4):
+            nc.scalar.activation(
+                out=junk[:], in_=raw1[:, t * D : (t + 1) * D], func=ACT.Copy, accum_out=wsum[:, t : t + 1]
+            )
+        nc.vector.tensor_reduce(
+            out=wsum[:, 0:2], in_=raw1[:, 0 : 2 * D].rearrange("p (t d) -> p t d", t=2), axis=AX.X, op=ALU.add
+        )
+        nc.vector.tensor_copy(out=wb[:], in_=wsum[:])
 
         raw2w = raw2[:].bitcast(F32)
         for g in range(2):
-            ps2 = psum_ht.tile([P, 512], F32, name="ps2", tag="ht")
+            ps2 = psum_ac.tile([P, 512], F32, name="ps2", tag="ac")
             for tt in range(2):
                 t = 2 * g + tt
                 for u in range(2):
@@ -260,39 +235,45 @@ def tile_divergencefreemlp_pa_t_kernel(tc, h1, h2, W1, W2, W3, out):
         raw2v = raw2[:].rearrange("p (t q s) -> p t q s", t=4, q=P, s=4)
         for s in range(4):
             lo = 2048 + s * H
-            nc.gpsimd.tensor_scalar(
-                out=gw[:, lo : lo + H].rearrange("p (q t) -> p q t", t=4),
-                in0=raw2v[:, :, :, s].rearrange("p t q -> p q t"),
-                scalar1=1.0,
-                scalar2=0.0,
-                op0=ALU.mult,
-                op1=ALU.add,
-            )
-        for k in range(1, LM + LT):
-            transposes(k)
-        for k in range(1, LM):
-            make_mask(k)
+            regrouped = gw[:, lo : lo + H].rearrange("p (q t) -> p q t", t=4)
+            rows = raw2v[:, :, :, s].rearrange("p t q -> p q t")
+            if s in (0, 1, 2):
+                nc.gpsimd.tensor_scalar(
+                    out=regrouped, in0=rows, scalar1=1.0, scalar2=0.0, op0=ALU.mult, op1=ALU.add
+                )
+            else:
+                nc.scalar.copy(out=regrouped, in_=rows)
+        nc.gpsimd.tensor_scalar(
+            out=gw[:, 5120:6144].rearrange("p (d t) -> p d t", t=4),
+            in0=raw1[:].rearrange("p (t d) -> p d t", t=4),
+            scalar1=-1.0,
+            scalar2=0.0,
+            op0=ALU.mult,
+            op1=ALU.add,
+        )
+        nc.scalar.copy(
+            out=gww[:, 2048:2560].rearrange("p (c u) -> p c u", u=2),
+            in_=ps3[:].rearrange("p (u c) -> p c u", u=2),
+        )
 
-        for i in range(NR + LA + LO):
-            if 0 <= i - 1 < NR:
-                first_matmuls(i - 1)
-            if 0 <= i - LA - LO < NR:
-                last_matmuls(i - LA - LO)
-            if i + LM + LT < NR:
-                transposes(i + LM + LT)
-            if 0 <= i - LA < NR:
-                mask_ac(i - LA)
-            if i < NR:
-                make_up(i)
-            if i == 0:
+        make_mask(1)
+        for k in range(NCH + L + 1):
+            if k + 1 < NCH:
+                transposes(k + 1)
+            if k < NCH:
+                make_up(k)
+            if k == 1:
                 quantise_weights(0)
-            if 0 <= i - LA < NR:
-                accodes[i - LA] = quantise(acms[i - LA], SIZES[i - LA], "ac")
-            if i < NR:
-                upcodes[i] = quantise(ups[i], SIZES[i], "up")
-            if i == 0:
                 quantise_weights(1)
-            if i + LM < NR:
-                make_mask(i + LM)
-            if i == 0:
+            if k + 2 < NCH:
+                make_mask(k + 2)
+            if k >= 1:
+                quantise(k - 1)
+                if k - 1 < NCH:
+                    first_matmuls(k - 1)
+                if k - 1 >= L:
+                    last_matmuls(k - 1 - L)
+            if k == 2:
                 quantise_weights(2)
+            if 0 <= k - L < NCH:
+                mask_ac(k - L)

@@ -20,6 +20,7 @@ H = 512
 D = 256
 NCH = B // P
 GROUPS = [1, 1, 2, 4, 4, 4, 4, 4, 4, 4]
+S_PAIRS = (12, 20, 28)
 L = 3
 
 
@@ -50,11 +51,12 @@ def tile_divergencefreemlp_pa_t_kernel(tc, h1, h2, W1, W2, W3, out):
                 where[n0 + l] = (hs, ln, l)
             n0 += ln
             if g == 0:
+                nc.sync.dma_start(out=raw1[:], in_=W1.rearrange("(p t) d -> p (t d)", t=4))
                 nc.sync.dma_start(
                     out=raw3[:].rearrange("p (t i) -> p t i", t=2),
                     in_=W3.rearrange("(t p) i -> p t i", p=P),
                 )
-                nc.sync.dma_start(out=raw1[:], in_=W1.rearrange("(p t) d -> p (t d)", t=4))
+            if g == 1:
                 nc.sync.dma_start(out=raw2[:], in_=W2.rearrange("(p t) j -> p (t j)", t=4))
         outv = out.rearrange("(p n) d -> p n d", n=NCH)
 
@@ -71,36 +73,59 @@ def tile_divergencefreemlp_pa_t_kernel(tc, h1, h2, W1, W2, W3, out):
         junk = const.tile([P, D], BF16, name="junk")
 
         mnat = {}
+        stiles = {}
         mtiles = {}
         pairs = {}
-        codes = {}
+        ucodes = {}
+        accodes = {}
         acbs = {}
 
-        def make_mask(k):
+        def make_mask(k, n):
             hs, ln, l = where[k]
-            hc = hs[:].rearrange("p (x n j) -> p x n j", x=2, n=ln)[:, :, l, :]
-            m = work.tile([P, 2 * H], BF16, name="mask", tag="mask", bufs=4)
+            m = work.tile([P, 2 * n * H], BF16, name="mask%d" % n, tag="mask%d" % n, bufs=3)
             nc.vector.tensor_single_scalar(
-                out=m[:].rearrange("p (x j) -> p x j", x=2), in_=hc, scalar=0.0, op=ALU.is_gt
+                out=m[:].rearrange("p (x n j) -> p x n j", x=2, n=n),
+                in_=hs[:].rearrange("p (x n j) -> p x n j", x=2, n=ln)[:, :, l : l + n, :],
+                scalar=0.0,
+                op=ALU.is_gt,
             )
-            mnat[k] = m
+            for i in range(n):
+                mnat[k + i] = [m[:, (x * n + i) * H : (x * n + i + 1) * H].bitcast(F32) for x in range(2)]
+
+        def mask_piece_scalar(k, c, second):
+            hs, ln, l = where[k]
+            if k not in stiles:
+                stiles[k] = (
+                    work.tile([P, 4 * H], BF16, name="rl", tag="rl", bufs=1),
+                    work.tile([P, 4 * H], BF16, name="smask", tag="smask", bufs=1),
+                )
+            rl, m = stiles[k]
+            if second:
+                nc.scalar.activation(
+                    out=m[:, c * 2 * H : (c + 1) * 2 * H], in_=rl[:, c * 2 * H : (c + 1) * 2 * H], func=ACT.Sign
+                )
+                mnat[k + c] = [m[:, (2 * c + x) * H : (2 * c + x + 1) * H].bitcast(F32) for x in range(2)]
+            else:
+                nc.scalar.activation(
+                    out=rl[:, c * 2 * H : (c + 1) * 2 * H].rearrange("p (x j) -> p x j", x=2),
+                    in_=hs[:].rearrange("p (x n j) -> p x n j", x=2, n=ln)[:, :, l + c, :],
+                    func=ACT.Relu,
+                )
 
         def transposes(k):
-            w = mnat[k][:].bitcast(F32)
             bank = psum_m.tile([P, 512], F32, name="m", tag="m")
             for x in range(2):
-                lo = x * 256
                 for u in range(2):
                     nc.tensor.transpose(
                         out=bank[:, (2 * u + x) * P : (2 * u + x + 1) * P],
-                        in_=w[:, lo + u : lo + 256 : 2],
+                        in_=mnat[k][x][:, u : 256 : 2],
                         identity=ident[:],
                     )
             mtiles[k] = bank[:].bitcast(BF16).rearrange("p (u x b e) -> p x b u e", u=2, x=2, e=2)
 
         def pair(k):
             if k not in pairs:
-                pairs[k] = work.tile([P, 4 * H], BF16, name="pair", tag="pair", bufs=3, align_bytes=64)
+                pairs[k] = work.tile([P, 4 * H], BF16, name="pair", tag="pair", bufs=4, align_bytes=64)
             return pairs[k]
 
         def make_up(k):
@@ -119,21 +144,22 @@ def tile_divergencefreemlp_pa_t_kernel(tc, h1, h2, W1, W2, W3, out):
                 op=ALU.mult,
             )
 
-        def quantise(k):
-            cd = work.tile([P, 4 * P], U32, name="cd", tag="cd", bufs=3, align_bytes=64)
-            sc = work.tile([P, 4 * P], U8, name="sc", tag="sc", bufs=3, align_bytes=64)
-            lo = 0 if k < NCH else 2
-            hi = 4 if k >= L else 2
+        def quantise(k, lo, hi):
+            cd = work.tile([P, 4 * P], U32, name="cd", tag="cd", bufs=4, align_bytes=64)
+            sc = work.tile([P, 4 * P], U8, name="sc", tag="sc", bufs=4, align_bytes=64)
             nc.vector.quantize_mx(
                 out=cd[:, lo * P : hi * P].bitcast(FP8X4),
                 scales=sc[:, lo * P : hi * P],
                 in_=pair(k)[:, lo * H : hi * H],
             )
-            codes[k] = (cd, sc)
+            if lo == 0:
+                ucodes[k] = (cd, sc)
+            if hi == 4:
+                accodes[k - L] = (cd, sc)
 
         def first_matmuls(k):
-            cd, sc = codes[k]
-            acb = work.tile([P, 2 * H], BF16, name="acb", tag="acb", bufs=3)
+            cd, sc = ucodes[k]
+            acb = work.tile([P, 2 * H], BF16, name="acb", tag="acb", bufs=4)
             for xin in range(2):
                 xo = 1 - xin
                 ps = psum_ac.tile([P, 512], F32, name="ac", tag="ac")
@@ -155,8 +181,11 @@ def tile_divergencefreemlp_pa_t_kernel(tc, h1, h2, W1, W2, W3, out):
             acbs[k] = acb
 
         def last_matmuls(k):
-            cd, sc = codes[k + L]
-            o = psum_o.tile([P, D], F32, name="o", tag="o")
+            cd, sc = accodes[k]
+            if k < NCH - L:
+                o = psum_o.tile([P, D], F32, name="o", tag="o")
+            else:
+                o = psum_m.tile([P, D], F32, name="ot", tag="m")
             nc.tensor.matmul_mx(
                 out=o[:],
                 lhsT=cd[:, 3 * P : 4 * P].bitcast(FP8X4),
@@ -186,7 +215,15 @@ def tile_divergencefreemlp_pa_t_kernel(tc, h1, h2, W1, W2, W3, out):
                 in_=gw[:, s * 2048 : (s + 1) * 2048],
             )
 
-        make_mask(0)
+        ps3 = psum_m.tile([P, 512], F32, name="ps3", tag="m")
+        make_mask(0, 1)
+        for t in range(2, 4):
+            nc.scalar.activation(
+                out=junk[:], in_=raw1[:, t * D : (t + 1) * D], func=ACT.Copy, accum_out=wsum[:, t : t + 1]
+            )
+        nc.vector.tensor_reduce(
+            out=wsum[:, 0:2], in_=raw1[:, 0 : 2 * D].rearrange("p (t d) -> p t d", t=2), axis=AX.X, op=ALU.add
+        )
         pw = psum_o.tile([P, D], F32, name="pw", tag="o")
         for t in range(4):
             for dh in range(2):
@@ -197,10 +234,12 @@ def tile_divergencefreemlp_pa_t_kernel(tc, h1, h2, W1, W2, W3, out):
                     start=dh == 0,
                     stop=dh == 1,
                 )
-        nc.scalar.copy(out=wsum[:, 4:8], in_=pw[:, 0:4])
-        raw3w = raw3[:].bitcast(F32)
-        ps3 = psum_m.tile([P, 512], F32, name="ps3", tag="m")
         transposes(0)
+        nc.scalar.copy(out=wsum[:, 4:8], in_=pw[:, 0:4])
+        make_mask(1, 1)
+        nc.vector.tensor_copy(out=wb[:], in_=wsum[:])
+        make_up(0)
+        raw3w = raw3[:].bitcast(F32)
         for dh in range(2):
             for u in range(2):
                 nc.tensor.transpose(
@@ -208,15 +247,21 @@ def tile_divergencefreemlp_pa_t_kernel(tc, h1, h2, W1, W2, W3, out):
                     in_=raw3w[:, dh * 256 + u : (dh + 1) * 256 : 2],
                     identity=ident[:],
                 )
-        for t in range(2, 4):
-            nc.scalar.activation(
-                out=junk[:], in_=raw1[:, t * D : (t + 1) * D], func=ACT.Copy, accum_out=wsum[:, t : t + 1]
-            )
-        nc.vector.tensor_reduce(
-            out=wsum[:, 0:2], in_=raw1[:, 0 : 2 * D].rearrange("p (t d) -> p t d", t=2), axis=AX.X, op=ALU.add
-        )
-        nc.vector.tensor_copy(out=wb[:], in_=wsum[:])
+        transposes(1)
+        quantise(0, 0, 2)
+        make_up(1)
 
+        raw2v = raw2[:].rearrange("p (t q s) -> p t q s", t=4, q=P, s=4)
+        for s in range(4):
+            lo = 2048 + s * H
+            regrouped = gw[:, lo : lo + H].rearrange("p (q t) -> p q t", t=4)
+            rows = raw2v[:, :, :, s].rearrange("p t q -> p q t")
+            if s in (0, 1):
+                nc.gpsimd.tensor_scalar(
+                    out=regrouped, in0=rows, scalar1=1.0, scalar2=0.0, op0=ALU.mult, op1=ALU.add
+                )
+            else:
+                nc.scalar.copy(out=regrouped, in_=rows)
         raw2w = raw2[:].bitcast(F32)
         for g in range(2):
             ps2 = psum_ac.tile([P, 512], F32, name="ps2", tag="ac")
@@ -232,17 +277,10 @@ def tile_divergencefreemlp_pa_t_kernel(tc, h1, h2, W1, W2, W3, out):
                 out=gww[:, g * 512 : (g + 1) * 512].rearrange("p (c u) -> p c u", u=2),
                 in_=ps2[:].rearrange("p (u c) -> p c u", u=2),
             )
-        raw2v = raw2[:].rearrange("p (t q s) -> p t q s", t=4, q=P, s=4)
-        for s in range(4):
-            lo = 2048 + s * H
-            regrouped = gw[:, lo : lo + H].rearrange("p (q t) -> p q t", t=4)
-            rows = raw2v[:, :, :, s].rearrange("p t q -> p q t")
-            if s in (0, 1, 2):
-                nc.gpsimd.tensor_scalar(
-                    out=regrouped, in0=rows, scalar1=1.0, scalar2=0.0, op0=ALU.mult, op1=ALU.add
-                )
-            else:
-                nc.scalar.copy(out=regrouped, in_=rows)
+        nc.scalar.copy(
+            out=gww[:, 2048:2560].rearrange("p (c u) -> p c u", u=2),
+            in_=ps3[:].rearrange("p (u c) -> p c u", u=2),
+        )
         nc.gpsimd.tensor_scalar(
             out=gw[:, 5120:6144].rearrange("p (d t) -> p d t", t=4),
             in0=raw1[:].rearrange("p (t d) -> p d t", t=4),
@@ -251,29 +289,42 @@ def tile_divergencefreemlp_pa_t_kernel(tc, h1, h2, W1, W2, W3, out):
             op0=ALU.mult,
             op1=ALU.add,
         )
-        nc.scalar.copy(
-            out=gww[:, 2048:2560].rearrange("p (c u) -> p c u", u=2),
-            in_=ps3[:].rearrange("p (u c) -> p c u", u=2),
-        )
+        make_mask(2, 2)
+        transposes(2)
+        quantise(1, 0, 2)
+        quantise_weights(1)
+        make_up(2)
+        transposes(3)
+        quantise_weights(0)
+        first_matmuls(0)
+        make_mask(4, 2)
+        first_matmuls(1)
 
-        make_mask(1)
-        for k in range(NCH + L + 1):
-            if k + 1 < NCH:
-                transposes(k + 1)
-            if k < NCH:
-                make_up(k)
-            if k == 1:
-                quantise_weights(0)
-                quantise_weights(1)
-            if k + 2 < NCH:
-                make_mask(k + 2)
-            if k >= 1:
-                quantise(k - 1)
-                if k - 1 < NCH:
-                    first_matmuls(k - 1)
-                if k - 1 >= L:
-                    last_matmuls(k - 1 - L)
-            if k == 2:
+        for k in range(3, NCH - 1):
+            transposes(k + 1)
+            make_up(k)
+            if k % 2 == 0 and k + 2 < NCH and k + 2 not in S_PAIRS:
+                make_mask(k + 2, 2)
+            quantise(k - 1, 0, 4 if k - 1 >= L else 2)
+            first_matmuls(k - 1)
+            if k - 1 >= L:
+                last_matmuls(k - 1 - L)
+            if k == 3:
                 quantise_weights(2)
-            if 0 <= k - L < NCH:
-                mask_ac(k - L)
+            mask_ac(k - L)
+            for n0 in S_PAIRS:
+                if n0 - k in (9, 7, 5, 3):
+                    piece = (9 - n0 + k) // 2
+                    mask_piece_scalar(n0, piece % 2, piece >= 2)
+
+        k = NCH - 1
+        make_up(k)
+        quantise(k - 1, 0, 4)
+        first_matmuls(k - 1)
+        last_matmuls(k - 1 - L)
+        quantise(k, 0, 2)
+        first_matmuls(k)
+        for j in range(NCH - 1 - L, NCH):
+            mask_ac(j)
+            quantise(j + L, 2, 4)
+            last_matmuls(j)

@@ -51,11 +51,11 @@ def tile_divergencefreemlp_pa_t_kernel(tc, h1, h2, W1, W2, W3, out):
                 where[n0 + l] = (hs, ln, l)
             n0 += ln
             if g == 0:
-                nc.sync.dma_start(out=raw1[:], in_=W1.rearrange("(p t) d -> p (t d)", t=4))
                 nc.sync.dma_start(
                     out=raw3[:].rearrange("p (t i) -> p t i", t=2),
                     in_=W3.rearrange("(t p) i -> p t i", p=P),
                 )
+                nc.sync.dma_start(out=raw1[:], in_=W1.rearrange("(p t) d -> p (t d)", t=4))
             if g == 1:
                 nc.sync.dma_start(out=raw2[:], in_=W2.rearrange("(p t) j -> p (t j)", t=4))
         outv = out.rearrange("(p n) d -> p n d", n=NCH)
@@ -136,9 +136,9 @@ def tile_divergencefreemlp_pa_t_kernel(tc, h1, h2, W1, W2, W3, out):
                 op=ALU.mult,
             )
 
-        def mask_ac(k):
+        def mask_ac(k, dst):
             nc.vector.tensor_tensor(
-                out=pair(k + L)[:, 2 * H : 4 * H].rearrange("p (x b u e) -> p x b u e", x=2, u=2, e=2),
+                out=dst.rearrange("p (x b u e) -> p x b u e", x=2, u=2, e=2),
                 in0=mtiles[k],
                 in1=acbs[k][:].rearrange("p (x b u e) -> p x b u e", x=2, u=2, e=2),
                 op=ALU.mult,
@@ -155,7 +155,7 @@ def tile_divergencefreemlp_pa_t_kernel(tc, h1, h2, W1, W2, W3, out):
             if lo == 0:
                 ucodes[k] = (cd, sc)
             if hi == 4:
-                accodes[k - L] = (cd, sc)
+                accodes[k - L] = (cd, sc, 1)
 
         def first_matmuls(k):
             cd, sc = ucodes[k]
@@ -181,15 +181,16 @@ def tile_divergencefreemlp_pa_t_kernel(tc, h1, h2, W1, W2, W3, out):
             acbs[k] = acb
 
         def last_matmuls(k):
-            cd, sc = accodes[k]
-            if k < NCH - L:
+            cd, sc, half = accodes[k]
+            clo, alo = 2 * half * P, (2 * half + 1) * P
+            if k < NCH - L - 2:
                 o = psum_o.tile([P, D], F32, name="o", tag="o")
             else:
                 o = psum_m.tile([P, D], F32, name="ot", tag="m")
             nc.tensor.matmul_mx(
                 out=o[:],
-                lhsT=cd[:, 3 * P : 4 * P].bitcast(FP8X4),
-                lhsT_scale=sc[:, 3 * P : 4 * P],
+                lhsT=cd[:, alo : alo + P].bitcast(FP8X4),
+                lhsT_scale=sc[:, alo : alo + P],
                 rhs=wcodes[:, 1024:1280].bitcast(FP8X4),
                 rhs_scale=wscales[:, 1024:1280],
                 start=True,
@@ -197,14 +198,14 @@ def tile_divergencefreemlp_pa_t_kernel(tc, h1, h2, W1, W2, W3, out):
             )
             nc.tensor.matmul_mx(
                 out=o[:],
-                lhsT=cd[:, 2 * P : 3 * P].bitcast(FP8X4),
-                lhsT_scale=sc[:, 2 * P : 3 * P],
+                lhsT=cd[:, clo : clo + P].bitcast(FP8X4),
+                lhsT_scale=sc[:, clo : clo + P],
                 rhs=wcodes[:, 1280:1536].bitcast(FP8X4),
                 rhs_scale=wscales[:, 1280:1536],
                 start=False,
                 stop=True,
             )
-            osb = work.tile([P, D], F32, name="osb", tag="osb", bufs=4)
+            osb = work.tile([P, D], F32, name="osb", tag="osb", bufs=8)
             nc.scalar.copy(out=osb[:], in_=o[:])
             nc.sync.dma_start(out=outv[:, k, :], in_=osb[:])
 
@@ -239,6 +240,9 @@ def tile_divergencefreemlp_pa_t_kernel(tc, h1, h2, W1, W2, W3, out):
         make_mask(1, 1)
         nc.vector.tensor_copy(out=wb[:], in_=wsum[:])
         make_up(0)
+        transposes(1)
+        make_up(1)
+        quantise(0, 0, 2)
         raw3w = raw3[:].bitcast(F32)
         for dh in range(2):
             for u in range(2):
@@ -247,9 +251,6 @@ def tile_divergencefreemlp_pa_t_kernel(tc, h1, h2, W1, W2, W3, out):
                     in_=raw3w[:, dh * 256 + u : (dh + 1) * 256 : 2],
                     identity=ident[:],
                 )
-        transposes(1)
-        quantise(0, 0, 2)
-        make_up(1)
 
         raw2v = raw2[:].rearrange("p (t q s) -> p t q s", t=4, q=P, s=4)
         for s in range(4):
@@ -293,14 +294,14 @@ def tile_divergencefreemlp_pa_t_kernel(tc, h1, h2, W1, W2, W3, out):
         transposes(2)
         quantise(1, 0, 2)
         quantise_weights(1)
-        make_up(2)
-        transposes(3)
         quantise_weights(0)
+        transposes(3)
         first_matmuls(0)
-        make_mask(4, 2)
         first_matmuls(1)
+        make_up(2)
+        make_mask(4, 2)
 
-        for k in range(3, NCH - 1):
+        for k in range(3, NCH - 2):
             transposes(k + 1)
             make_up(k)
             if k % 2 == 0 and k + 2 < NCH and k + 2 not in S_PAIRS:
@@ -311,20 +312,41 @@ def tile_divergencefreemlp_pa_t_kernel(tc, h1, h2, W1, W2, W3, out):
                 last_matmuls(k - 1 - L)
             if k == 3:
                 quantise_weights(2)
-            mask_ac(k - L)
+            mask_ac(k - L, pair(k)[:, 2 * H : 4 * H])
             for n0 in S_PAIRS:
                 if n0 - k in (9, 7, 5, 3):
                     piece = (9 - n0 + k) // 2
                     mask_piece_scalar(n0, piece % 2, piece >= 2)
 
-        k = NCH - 1
+        k = NCH - 2
+        transposes(k + 1)
         make_up(k)
         quantise(k - 1, 0, 4)
         first_matmuls(k - 1)
         last_matmuls(k - 1 - L)
+        make_up(k + 1)
         quantise(k, 0, 2)
         first_matmuls(k)
-        for j in range(NCH - 1 - L, NCH):
-            mask_ac(j)
-            quantise(j + L, 2, 4)
-            last_matmuls(j)
+        quantise(k + 1, 0, 2)
+        first_matmuls(k + 1)
+        lasts = list(range(k - L, NCH))
+        filled = {}
+        for i, j in enumerate(lasts):
+            if i % 2 == 0:
+                tile_ac = work.tile([P, 4 * H], BF16, name="pair", tag="pair", bufs=4, align_bytes=64)
+            filled[j] = (tile_ac, i % 2)
+            mask_ac(j, tile_ac[:, i % 2 * 2 * H : (i % 2 + 1) * 2 * H])
+            if i in (2, 3, 4):
+                first = lasts[{2: 0, 3: 2, 4: 4}[i]]
+                src = filled[first][0]
+                width = 4 if i < 4 else 2
+                cd = work.tile([P, 4 * P], U32, name="cd", tag="cd", bufs=4, align_bytes=64)
+                sc = work.tile([P, 4 * P], U8, name="sc", tag="sc", bufs=4, align_bytes=64)
+                nc.vector.quantize_mx(
+                    out=cd[:, 0 : width * P].bitcast(FP8X4),
+                    scales=sc[:, 0 : width * P],
+                    in_=src[:, 0 : width * H],
+                )
+                for h in range(width // 2):
+                    accodes[first + h] = (cd, sc, h)
+                    last_matmuls(first + h)

@@ -20,7 +20,8 @@ H = 512
 D = 256
 NCH = B // P
 GROUPS = [1, 1, 2, 4, 4, 4, 4, 4, 4, 4]
-S_PAIRS = (12, 20, 28)
+S_PAIRS = (18, 30)
+S_STEPS = [k for k in range(5, 28) if k % 3 != 1]
 L = 3
 
 
@@ -73,6 +74,7 @@ def tile_divergencefreemlp_pa_t_kernel(tc, h1, h2, W1, W2, W3, out):
         junk = const.tile([P, D], BF16, name="junk")
 
         mnat = {}
+        otiles = {}
         stiles = {}
         mtiles = {}
         pairs = {}
@@ -92,25 +94,22 @@ def tile_divergencefreemlp_pa_t_kernel(tc, h1, h2, W1, W2, W3, out):
             for i in range(n):
                 mnat[k + i] = [m[:, (x * n + i) * H : (x * n + i + 1) * H].bitcast(F32) for x in range(2)]
 
-        def mask_piece_scalar(k, c, second):
+        def mask_piece_scalar(k, i):
             hs, ln, l = where[k]
             if k not in stiles:
                 stiles[k] = (
-                    work.tile([P, 4 * H], BF16, name="rl", tag="rl", bufs=1),
-                    work.tile([P, 4 * H], BF16, name="smask", tag="smask", bufs=1),
+                    work.tile([P, 4 * H], BF16, name="rl", tag="rl", bufs=2),
+                    work.tile([P, 4 * H], BF16, name="smask", tag="smask", bufs=2),
                 )
             rl, m = stiles[k]
-            if second:
-                nc.scalar.activation(
-                    out=m[:, c * 2 * H : (c + 1) * 2 * H], in_=rl[:, c * 2 * H : (c + 1) * 2 * H], func=ACT.Sign
-                )
-                mnat[k + c] = [m[:, (2 * c + x) * H : (2 * c + x + 1) * H].bitcast(F32) for x in range(2)]
+            c, x = i % 4 // 2, i % 2
+            q = (2 * c + x) * H
+            if i < 4:
+                hlo = (x * ln + l + c) * H
+                nc.scalar.activation(out=rl[:, q : q + H], in_=hs[:, hlo : hlo + H], func=ACT.Relu)
             else:
-                nc.scalar.activation(
-                    out=rl[:, c * 2 * H : (c + 1) * 2 * H].rearrange("p (x j) -> p x j", x=2),
-                    in_=hs[:].rearrange("p (x n j) -> p x n j", x=2, n=ln)[:, :, l + c, :],
-                    func=ACT.Relu,
-                )
+                nc.scalar.activation(out=m[:, q : q + H], in_=rl[:, q : q + H], func=ACT.Sign)
+                mnat.setdefault(k + c, []).append(m[:, q : q + H].bitcast(F32))
 
         def transposes(k):
             bank = psum_m.tile([P, 512], F32, name="m", tag="m")
@@ -155,7 +154,7 @@ def tile_divergencefreemlp_pa_t_kernel(tc, h1, h2, W1, W2, W3, out):
             if lo == 0:
                 ucodes[k] = (cd, sc)
             if hi == 4:
-                accodes[k - L] = (cd, sc, 1)
+                accodes[k - 1 - L] = (cd, sc, 1)
 
         def first_matmuls(k):
             cd, sc = ucodes[k]
@@ -183,12 +182,15 @@ def tile_divergencefreemlp_pa_t_kernel(tc, h1, h2, W1, W2, W3, out):
         def last_matmuls(k):
             cd, sc, half = accodes[k]
             clo, alo = 2 * half * P, (2 * half + 1) * P
-            if k < NCH - L - 2:
-                o = psum_o.tile([P, D], F32, name="o", tag="o")
+            if k >= 28:
+                otiles[k] = psum_m.tile([P, D], F32, name="ot", tag="m")
+                o = otiles[k][:]
             else:
-                o = psum_m.tile([P, D], F32, name="ot", tag="m")
+                if k % 2 == 0:
+                    otiles[k] = psum_o.tile([P, 2 * D], F32, name="o", tag="o")
+                o = otiles[k - k % 2][:, k % 2 * D : (k % 2 + 1) * D]
             nc.tensor.matmul_mx(
-                out=o[:],
+                out=o,
                 lhsT=cd[:, alo : alo + P].bitcast(FP8X4),
                 lhsT_scale=sc[:, alo : alo + P],
                 rhs=wcodes[:, 1024:1280].bitcast(FP8X4),
@@ -197,7 +199,7 @@ def tile_divergencefreemlp_pa_t_kernel(tc, h1, h2, W1, W2, W3, out):
                 stop=False,
             )
             nc.tensor.matmul_mx(
-                out=o[:],
+                out=o,
                 lhsT=cd[:, clo : clo + P].bitcast(FP8X4),
                 lhsT_scale=sc[:, clo : clo + P],
                 rhs=wcodes[:, 1280:1536].bitcast(FP8X4),
@@ -205,9 +207,14 @@ def tile_divergencefreemlp_pa_t_kernel(tc, h1, h2, W1, W2, W3, out):
                 start=False,
                 stop=True,
             )
-            osb = work.tile([P, D], F32, name="osb", tag="osb", bufs=8)
-            nc.scalar.copy(out=osb[:], in_=o[:])
-            nc.sync.dma_start(out=outv[:, k, :], in_=osb[:])
+            if k >= 28:
+                osb = work.tile([P, D], F32, name="ost", tag="ost", bufs=4)
+                nc.scalar.copy(out=osb[:], in_=otiles[k][:])
+                nc.sync.dma_start(out=outv[:, k, :], in_=osb[:])
+            elif k % 2 == 1:
+                osb = work.tile([P, 2 * D], F32, name="osb", tag="osb", bufs=6)
+                nc.scalar.copy(out=osb[:], in_=otiles[k - 1][:])
+                nc.sync.dma_start(out=outv[:, k - 1 : k + 1, :], in_=osb[:].rearrange("p (n d) -> p n d", n=2))
 
         def quantise_weights(s):
             nc.vector.quantize_mx(
@@ -225,7 +232,7 @@ def tile_divergencefreemlp_pa_t_kernel(tc, h1, h2, W1, W2, W3, out):
         nc.vector.tensor_reduce(
             out=wsum[:, 0:2], in_=raw1[:, 0 : 2 * D].rearrange("p (t d) -> p t d", t=2), axis=AX.X, op=ALU.add
         )
-        pw = psum_o.tile([P, D], F32, name="pw", tag="o")
+        pw = psum_o.tile([P, 2 * D], F32, name="pw", tag="o")
         for t in range(4):
             for dh in range(2):
                 nc.tensor.matmul(
@@ -252,15 +259,19 @@ def tile_divergencefreemlp_pa_t_kernel(tc, h1, h2, W1, W2, W3, out):
                     identity=ident[:],
                 )
 
+        nc.scalar.activation(
+            out=gw[:, 5120:6144].rearrange("p (d t) -> p d t", t=4),
+            in_=raw1[:].rearrange("p (t d) -> p d t", t=4),
+            func=ACT.Copy,
+            scale=-1.0,
+        )
         raw2v = raw2[:].rearrange("p (t q s) -> p t q s", t=4, q=P, s=4)
         for s in range(4):
             lo = 2048 + s * H
             regrouped = gw[:, lo : lo + H].rearrange("p (q t) -> p q t", t=4)
             rows = raw2v[:, :, :, s].rearrange("p t q -> p q t")
-            if s in (0, 1):
-                nc.gpsimd.tensor_scalar(
-                    out=regrouped, in0=rows, scalar1=1.0, scalar2=0.0, op0=ALU.mult, op1=ALU.add
-                )
+            if s in (2, 3):
+                nc.vector.tensor_copy(out=regrouped, in_=rows)
             else:
                 nc.scalar.copy(out=regrouped, in_=rows)
         raw2w = raw2[:].bitcast(F32)
@@ -282,14 +293,6 @@ def tile_divergencefreemlp_pa_t_kernel(tc, h1, h2, W1, W2, W3, out):
             out=gww[:, 2048:2560].rearrange("p (c u) -> p c u", u=2),
             in_=ps3[:].rearrange("p (u c) -> p c u", u=2),
         )
-        nc.gpsimd.tensor_scalar(
-            out=gw[:, 5120:6144].rearrange("p (d t) -> p d t", t=4),
-            in0=raw1[:].rearrange("p (t d) -> p d t", t=4),
-            scalar1=-1.0,
-            scalar2=0.0,
-            op0=ALU.mult,
-            op1=ALU.add,
-        )
         make_mask(2, 2)
         transposes(2)
         quantise(1, 0, 2)
@@ -302,31 +305,31 @@ def tile_divergencefreemlp_pa_t_kernel(tc, h1, h2, W1, W2, W3, out):
         make_mask(4, 2)
 
         for k in range(3, NCH - 2):
+            quantise(k - 1, 0, 4 if k - 2 >= L else 2)
             transposes(k + 1)
+            first_matmuls(k - 1)
+            if k - 2 >= L:
+                last_matmuls(k - 2 - L)
             make_up(k)
             if k % 2 == 0 and k + 2 < NCH and k + 2 not in S_PAIRS:
                 make_mask(k + 2, 2)
-            quantise(k - 1, 0, 4 if k - 1 >= L else 2)
-            first_matmuls(k - 1)
-            if k - 1 >= L:
-                last_matmuls(k - 1 - L)
             if k == 3:
                 quantise_weights(2)
-            mask_ac(k - L, pair(k)[:, 2 * H : 4 * H])
-            for n0 in S_PAIRS:
-                if n0 - k in (9, 7, 5, 3):
-                    piece = (9 - n0 + k) // 2
-                    mask_piece_scalar(n0, piece % 2, piece >= 2)
+            mask_ac(k - L, pair(k + 1)[:, 2 * H : 4 * H])
+            if k in S_STEPS:
+                i = S_STEPS.index(k)
+                mask_piece_scalar(S_PAIRS[i // 8], i % 8)
 
         k = NCH - 2
-        transposes(k + 1)
-        make_up(k)
         quantise(k - 1, 0, 4)
+        transposes(k + 1)
         first_matmuls(k - 1)
-        last_matmuls(k - 1 - L)
+        last_matmuls(k - 2 - L)
+        make_up(k)
         make_up(k + 1)
-        quantise(k, 0, 2)
+        quantise(k, 0, 4)
         first_matmuls(k)
+        last_matmuls(k - 1 - L)
         quantise(k + 1, 0, 2)
         first_matmuls(k + 1)
         lasts = list(range(k - L, NCH))

@@ -20,8 +20,9 @@ H = 512
 D = 256
 NCH = B // P
 GROUPS = [1, 1, 2, 4, 4, 4, 4, 4, 4, 4]
-S_PAIRS = (18, 30)
-S_STEPS = [k for k in range(5, 28) if k % 3 != 1]
+V_MASKS = {6: 2, 8: 4, 12: 2, 16: 4, 20: 2, 24: 4, 28: 2}
+S_PAIRS = (14, 22, 30)
+S_STEPS = [k for k in range(5, 29)]
 L = 3
 
 
@@ -52,11 +53,11 @@ def tile_divergencefreemlp_pa_t_kernel(tc, h1, h2, W1, W2, W3, out):
                 where[n0 + l] = (hs, ln, l)
             n0 += ln
             if g == 0:
+                nc.sync.dma_start(out=raw1[:], in_=W1.rearrange("(p t) d -> p (t d)", t=4))
                 nc.sync.dma_start(
                     out=raw3[:].rearrange("p (t i) -> p t i", t=2),
                     in_=W3.rearrange("(t p) i -> p t i", p=P),
                 )
-                nc.sync.dma_start(out=raw1[:], in_=W1.rearrange("(p t) d -> p (t d)", t=4))
             if g == 1:
                 nc.sync.dma_start(out=raw2[:], in_=W2.rearrange("(p t) j -> p (t j)", t=4))
         outv = out.rearrange("(p n) d -> p n d", n=NCH)
@@ -69,7 +70,7 @@ def tile_divergencefreemlp_pa_t_kernel(tc, h1, h2, W1, W2, W3, out):
         gww = gw[:].bitcast(F32)
         wcodes = const.tile([P, 1536], U32, name="wcodes", align_bytes=64)
         wscales = const.tile([P, 1536], U8, name="wscales", align_bytes=64)
-        wsum = const.tile([P, 8], F32, name="wsum")
+        wsum = const.tile([P, 4], F32, name="wsum")
         wb = const.tile([P, 8], BF16, name="wb")
         junk = const.tile([P, D], BF16, name="junk")
 
@@ -243,9 +244,9 @@ def tile_divergencefreemlp_pa_t_kernel(tc, h1, h2, W1, W2, W3, out):
                     stop=dh == 1,
                 )
         transposes(0)
-        nc.scalar.copy(out=wsum[:, 4:8], in_=pw[:, 0:4])
         make_mask(1, 1)
-        nc.vector.tensor_copy(out=wb[:], in_=wsum[:])
+        nc.vector.tensor_copy(out=wb[:, 0:4], in_=wsum[:])
+        nc.vector.tensor_copy(out=wb[:, 4:8], in_=pw[:, 0:4])
         make_up(0)
         transposes(1)
         make_up(1)
@@ -270,7 +271,7 @@ def tile_divergencefreemlp_pa_t_kernel(tc, h1, h2, W1, W2, W3, out):
             lo = 2048 + s * H
             regrouped = gw[:, lo : lo + H].rearrange("p (q t) -> p q t", t=4)
             rows = raw2v[:, :, :, s].rearrange("p t q -> p q t")
-            if s in (2, 3):
+            if s in (3,):
                 nc.vector.tensor_copy(out=regrouped, in_=rows)
             else:
                 nc.scalar.copy(out=regrouped, in_=rows)
@@ -311,8 +312,8 @@ def tile_divergencefreemlp_pa_t_kernel(tc, h1, h2, W1, W2, W3, out):
             if k - 2 >= L:
                 last_matmuls(k - 2 - L)
             make_up(k)
-            if k % 2 == 0 and k + 2 < NCH and k + 2 not in S_PAIRS:
-                make_mask(k + 2, 2)
+            if k + 2 in V_MASKS:
+                make_mask(k + 2, V_MASKS[k + 2])
             if k == 3:
                 quantise_weights(2)
             mask_ac(k - L, pair(k + 1)[:, 2 * H : 4 * H])

@@ -117,11 +117,11 @@ def tile_divergencefreemlp_pa_t_kernel(tc, h1, h2, W1, W2, W3, out):
             for x in range(2):
                 for u in range(2):
                     nc.tensor.transpose(
-                        out=bank[:, (2 * u + x) * P : (2 * u + x + 1) * P],
+                        out=bank[:, x * 256 + u : (x + 1) * 256 : 2],
                         in_=mnat[k][x][:, u : 256 : 2],
                         identity=ident[:],
                     )
-            mtiles[k] = bank[:].bitcast(BF16).rearrange("p (u x b e) -> p x b u e", u=2, x=2, e=2)
+            mtiles[k] = bank[:].bitcast(BF16).rearrange("p (x b u e) -> p x b u e", u=2, x=2, e=2)
 
         def pair(k):
             if k not in pairs:

@@ -20,9 +20,9 @@ H = 512
 D = 256
 NCH = B // P
 GROUPS = [1, 1, 2, 4, 4, 4, 4, 4, 4, 4]
-V_MASKS = {6: 2, 8: 4, 12: 2, 16: 4, 20: 2, 24: 4, 28: 2}
-S_PAIRS = (14, 22, 30)
-S_STEPS = [k for k in range(5, 29)]
+V_MASKS = {6: 1, 8: 4, 12: 2, 16: 4, 20: 2, 24: 4, 28: 2}
+S_CHUNKS = (7, 14, 15, 22, 23, 30, 31)
+S_STEPS = list(range(3, 29))
 L = 3
 
 
@@ -95,22 +95,23 @@ def tile_divergencefreemlp_pa_t_kernel(tc, h1, h2, W1, W2, W3, out):
             for i in range(n):
                 mnat[k + i] = [m[:, (x * n + i) * H : (x * n + i + 1) * H].bitcast(F32) for x in range(2)]
 
-        def mask_piece_scalar(k, i):
+        def mask_piece_scalar(i):
+            k, x = S_CHUNKS[i // 4], i % 2
             hs, ln, l = where[k]
-            if k not in stiles:
+            if i % 4 == 0:
                 stiles[k] = (
-                    work.tile([P, 4 * H], BF16, name="rl", tag="rl", bufs=2),
-                    work.tile([P, 4 * H], BF16, name="smask", tag="smask", bufs=2),
+                    work.tile([P, 2 * H], BF16, name="rl", tag="rl", bufs=2),
+                    work.tile([P, 2 * H], BF16, name="smask", tag="smask", bufs=3),
                 )
             rl, m = stiles[k]
-            c, x = i % 4 // 2, i % 2
-            q = (2 * c + x) * H
-            if i < 4:
-                hlo = (x * ln + l + c) * H
-                nc.scalar.activation(out=rl[:, q : q + H], in_=hs[:, hlo : hlo + H], func=ACT.Relu)
+            if i % 4 < 2:
+                lo = (x * ln + l) * H
+                nc.scalar.activation(out=rl[:, x * H : (x + 1) * H], in_=hs[:, lo : lo + H], func=ACT.Relu)
             else:
-                nc.scalar.activation(out=m[:, q : q + H], in_=rl[:, q : q + H], func=ACT.Sign)
-                mnat.setdefault(k + c, []).append(m[:, q : q + H].bitcast(F32))
+                nc.scalar.activation(
+                    out=m[:, x * H : (x + 1) * H], in_=rl[:, x * H : (x + 1) * H], func=ACT.Sign
+                )
+                mnat.setdefault(k, []).append(m[:, x * H : (x + 1) * H].bitcast(F32))
 
         def transposes(k):
             bank = psum_m.tile([P, 512], F32, name="m", tag="m")
@@ -294,6 +295,8 @@ def tile_divergencefreemlp_pa_t_kernel(tc, h1, h2, W1, W2, W3, out):
             out=gww[:, 2048:2560].rearrange("p (c u) -> p c u", u=2),
             in_=ps3[:].rearrange("p (u c) -> p c u", u=2),
         )
+        mask_piece_scalar(0)
+        mask_piece_scalar(1)
         make_mask(2, 2)
         transposes(2)
         quantise(1, 0, 2)
@@ -318,8 +321,7 @@ def tile_divergencefreemlp_pa_t_kernel(tc, h1, h2, W1, W2, W3, out):
                 quantise_weights(2)
             mask_ac(k - L, pair(k + 1)[:, 2 * H : 4 * H])
             if k in S_STEPS:
-                i = S_STEPS.index(k)
-                mask_piece_scalar(S_PAIRS[i // 8], i % 8)
+                mask_piece_scalar(S_STEPS.index(k) + 2)
 
         k = NCH - 2
         quantise(k - 1, 0, 4)

from contextlib import ExitStack

import concourse.mybir as mybir
from concourse.masks import make_identity

FLOPS = 2 * 4096 * 512 * 512 * 2 + 2 * 4096 * 512 * 256 * 2

FP8X4 = mybir.dt.float8_e4m3fn_x4
BF16 = mybir.dt.bfloat16
F32 = mybir.dt.float32
U32 = mybir.dt.uint32
U8 = mybir.dt.uint8
ALU = mybir.AluOpType
ACT = mybir.ActivationFunctionType
AX = mybir.AxisListType

P = 128
B = 4096
H = 512
D = 256
NCH = B // P
GROUPS = [1, 1, 2, 4, 4, 4, 4, 4, 4, 4]
V_MASKS = {6: 1, 8: 4, 12: 2, 16: 4, 20: 2, 24: 4, 28: 2}
S_CHUNKS = (7, 14, 15, 22, 23, 30, 31)
S_STEPS = list(range(3, 29))
L = 3


def tile_divergencefreemlp_pa_t_kernel(tc, h1, h2, W1, W2, W3, out):
    nc = tc.nc
    with ExitStack() as ctx:
        const = ctx.enter_context(tc.tile_pool(name="const", bufs=1))
        work = ctx.enter_context(tc.tile_pool(name="work", bufs=3))
        psum_m = ctx.enter_context(tc.psum_pool(name="psum_m", bufs=5))
        psum_ac = ctx.enter_context(tc.psum_pool(name="psum_ac", bufs=2))
        psum_o = ctx.enter_context(tc.psum_pool(name="psum_o", bufs=1))
        ctx.enter_context(tc.manual_schedule())

        raw1 = const.tile([P, 4 * D], BF16, name="raw1")
        raw3 = const.tile([P, 2 * H], BF16, name="raw3")
        raw2 = const.tile([P, 4 * H], BF16, name="raw2")
        hv = [h1.rearrange("(p n) j -> p n j", n=NCH), h2.rearrange("(p n) j -> p n j", n=NCH)]
        where = {}
        n0 = 0
        for g, ln in enumerate(GROUPS):
            hs = const.tile([P, 2 * ln * H], BF16, name="h_%d" % g)
            for x in range(2):
                nc.sync.dma_start(
                    out=hs[:, x * ln * H : (x + 1) * ln * H].rearrange("p (n j) -> p n j", n=ln),
                    in_=hv[x][:, n0 : n0 + ln, :],
                )
            for l in range(ln):
                where[n0 + l] = (hs, ln, l)
            n0 += ln
            if g == 0:
                nc.sync.dma_start(out=raw1[:], in_=W1.rearrange("(p t) d -> p (t d)", t=4))
                nc.sync.dma_start(
                    out=raw3[:].rearrange("p (t i) -> p t i", t=2),
                    in_=W3.rearrange("(t p) i -> p t i", p=P),
                )
            if g == 1:
                nc.sync.dma_start(out=raw2[:], in_=W2.rearrange("(p t) j -> p (t j)", t=4))
        outv = out.rearrange("(p n) d -> p n d", n=NCH)

        ident = const.tile([P, P], F32, name="ident")
        make_identity(nc, ident[:])
        ones = const.tile([P, 1], BF16, name="ones")
        nc.vector.memset(ones[:], 1.0)
        gw = const.tile([P, 6144], BF16, name="gw", align_bytes=64)
        gww = gw[:].bitcast(F32)
        wcodes = const.tile([P, 1536], U32, name="wcodes", align_bytes=64)
        wscales = const.tile([P, 1536], U8, name="wscales", align_bytes=64)
        wsum = const.tile([P, 4], F32, name="wsum")
        wb = const.tile([P, 8], BF16, name="wb")
        junk = const.tile([P, D], BF16, name="junk")

        mnat = {}
        otiles = {}
        stiles = {}
        mtiles = {}
        pairs = {}
        ucodes = {}
        accodes = {}
        acbs = {}

        def make_mask(k, n):
            hs, ln, l = where[k]
            m = work.tile([P, 2 * n * H], BF16, name="mask%d" % n, tag="mask%d" % n, bufs=3)
            nc.vector.tensor_single_scalar(
                out=m[:].rearrange("p (x n j) -> p x n j", x=2, n=n),
                in_=hs[:].rearrange("p (x n j) -> p x n j", x=2, n=ln)[:, :, l : l + n, :],
                scalar=0.0,
                op=ALU.is_gt,
            )
            for i in range(n):
                mnat[k + i] = [m[:, (x * n + i) * H : (x * n + i + 1) * H].bitcast(F32) for x in range(2)]

        def mask_piece_scalar(i):
            k, x = S_CHUNKS[i // 4], i % 2
            hs, ln, l = where[k]
            if i % 4 == 0:
                stiles[k] = (
                    work.tile([P, 2 * H], BF16, name="rl", tag="rl", bufs=2),
                    work.tile([P, 2 * H], BF16, name="smask", tag="smask", bufs=3),
                )
            rl, m = stiles[k]
            if i % 4 < 2:
                lo = (x * ln + l) * H
                nc.scalar.activation(out=rl[:, x * H : (x + 1) * H], in_=hs[:, lo : lo + H], func=ACT.Relu)
            else:
                nc.scalar.activation(
                    out=m[:, x * H : (x + 1) * H], in_=rl[:, x * H : (x + 1) * H], func=ACT.Sign
                )
                mnat.setdefault(k, []).append(m[:, x * H : (x + 1) * H].bitcast(F32))

        def transposes(k):
            bank = psum_m.tile([P, 512], F32, name="m", tag="m")
            for x in range(2):
                for u in range(2):
                    nc.tensor.transpose(
                        out=bank[:, x * 256 + u : (x + 1) * 256 : 2],
                        in_=mnat[k][x][:, u : 256 : 2],
                        identity=ident[:],
                    )
            mtiles[k] = bank[:].bitcast(BF16).rearrange("p (x b u e) -> p x b u e", u=2, x=2, e=2)

        def pair(k):
            if k not in pairs:
                pairs[k] = work.tile([P, 4 * H], BF16, name="pair", tag="pair", bufs=4, align_bytes=64)
            return pairs[k]

        def make_up(k):
            nc.vector.tensor_tensor(
                out=pair(k)[:, 0 : 2 * H].rearrange("p (x b u e) -> p x b u e", x=2, u=2, e=2),
                in0=mtiles[k],
                in1=wb[:].rearrange("p (x u e) -> p x u e", x=2, u=2).unsqueeze(2).to_broadcast([P, 2, P, 2, 2]),
                op=ALU.mult,
            )

        def mask_ac(k, dst):
            nc.vector.tensor_tensor(
                out=dst.rearrange("p (x b u e) -> p x b u e", x=2, u=2, e=2),
                in0=mtiles[k],
                in1=acbs[k][:].rearrange("p (x b u e) -> p x b u e", x=2, u=2, e=2),
                op=ALU.mult,
            )

        def quantise(k, lo, hi):
            cd = work.tile([P, 4 * P], U32, name="cd", tag="cd", bufs=4, align_bytes=64)
            sc = work.tile([P, 4 * P], U8, name="sc", tag="sc", bufs=4, align_bytes=64)
            nc.vector.quantize_mx(
                out=cd[:, lo * P : hi * P].bitcast(FP8X4),
                scales=sc[:, lo * P : hi * P],
                in_=pair(k)[:, lo * H : hi * H],
            )
            if lo == 0:
                ucodes[k] = (cd, sc)
            if hi == 4:
                accodes[k - 1 - L] = (cd, sc, 1)

        def first_matmuls(k):
            cd, sc = ucodes[k]
            acb = work.tile([P, 2 * H], BF16, name="acb", tag="acb", bufs=4)
            for xin in range(2):
                xo = 1 - xin
                ps = psum_ac.tile([P, 512], F32, name="ac", tag="ac")
                for t in range(4):
                    wlo = 512 * xin + t * P
                    nc.tensor.matmul_mx(
                        out=ps[:, t * P : (t + 1) * P],
                        lhsT=wcodes[:, wlo : wlo + P].bitcast(FP8X4),
                        lhsT_scale=wscales[:, wlo : wlo + P],
                        rhs=cd[:, xin * P : (xin + 1) * P].bitcast(FP8X4),
                        rhs_scale=sc[:, xin * P : (xin + 1) * P],
                        start=True,
                        stop=True,
                    )
                nc.scalar.copy(
                    out=acb[:, xo * H : (xo + 1) * H].rearrange("p (b t) -> p b t", t=4),
                    in_=ps[:].rearrange("p (t b) -> p b t", t=4),
                )
            acbs[k] = acb

        def last_matmuls(k):
            cd, sc, half = accodes[k]
            clo, alo = 2 * half * P, (2 * half + 1) * P
            if k >= 28:
                otiles[k] = psum_m.tile([P, D], F32, name="ot", tag="m")
                o = otiles[k][:]
            else:
                if k % 2 == 0:
                    otiles[k] = psum_o.tile([P, 2 * D], F32, name="o", tag="o")
                o = otiles[k - k % 2][:, k % 2 * D : (k % 2 + 1) * D]
            nc.tensor.matmul_mx(
                out=o,
                lhsT=cd[:, alo : alo + P].bitcast(FP8X4),
                lhsT_scale=sc[:, alo : alo + P],
                rhs=wcodes[:, 1024:1280].bitcast(FP8X4),
                rhs_scale=wscales[:, 1024:1280],
                start=True,
                stop=False,
            )
            nc.tensor.matmul_mx(
                out=o,
                lhsT=cd[:, clo : clo + P].bitcast(FP8X4),
                lhsT_scale=sc[:, clo : clo + P],
                rhs=wcodes[:, 1280:1536].bitcast(FP8X4),
                rhs_scale=wscales[:, 1280:1536],
                start=False,
                stop=True,
            )
            if k >= 28:
                osb = work.tile([P, D], F32, name="ost", tag="ost", bufs=4)
                nc.scalar.copy(out=osb[:], in_=otiles[k][:])
                nc.sync.dma_start(out=outv[:, k, :], in_=osb[:])
            elif k % 2 == 1:
                osb = work.tile([P, 2 * D], F32, name="osb", tag="osb", bufs=6)
                nc.scalar.copy(out=osb[:], in_=otiles[k - 1][:])
                nc.sync.dma_start(out=outv[:, k - 1 : k + 1, :], in_=osb[:].rearrange("p (n d) -> p n d", n=2))

        def quantise_weights(s):
            nc.vector.quantize_mx(
                out=wcodes[:, s * 512 : (s + 1) * 512].bitcast(FP8X4),
                scales=wscales[:, s * 512 : (s + 1) * 512],
                in_=gw[:, s * 2048 : (s + 1) * 2048],
            )

        ps3 = psum_m.tile([P, 512], F32, name="ps3", tag="m")
        make_mask(0, 1)
        for t in range(2, 4):
            nc.scalar.activation(
                out=junk[:], in_=raw1[:, t * D : (t + 1) * D], func=ACT.Copy, accum_out=wsum[:, t : t + 1]
            )
        nc.vector.tensor_reduce(
            out=wsum[:, 0:2], in_=raw1[:, 0 : 2 * D].rearrange("p (t d) -> p t d", t=2), axis=AX.X, op=ALU.add
        )
        pw = psum_o.tile([P, 2 * D], F32, name="pw", tag="o")
        for t in range(4):
            for dh in range(2):
                nc.tensor.matmul(
                    out=pw[:, t : t + 1],
                    lhsT=raw3[:, dh * H + t : (dh + 1) * H : 4],
                    rhs=ones[:],
                    start=dh == 0,
                    stop=dh == 1,
                )
        transposes(0)
        make_mask(1, 1)
        nc.vector.tensor_copy(out=wb[:, 0:4], in_=wsum[:])
        nc.vector.tensor_copy(out=wb[:, 4:8], in_=pw[:, 0:4])
        make_up(0)
        transposes(1)
        make_up(1)
        quantise(0, 0, 2)
        raw3w = raw3[:].bitcast(F32)
        for dh in range(2):
            for u in range(2):
                nc.tensor.transpose(
                    out=ps3[:, u * 256 + dh * P : u * 256 + (dh + 1) * P],
                    in_=raw3w[:, dh * 256 + u : (dh + 1) * 256 : 2],
                    identity=ident[:],
                )

        nc.scalar.activation(
            out=gw[:, 5120:6144].rearrange("p (d t) -> p d t", t=4),
            in_=raw1[:].rearrange("p (t d) -> p d t", t=4),
            func=ACT.Copy,
            scale=-1.0,
        )
        raw2v = raw2[:].rearrange("p (t q s) -> p t q s", t=4, q=P, s=4)
        for s in range(4):
            lo = 2048 + s * H
            regrouped = gw[:, lo : lo + H].rearrange("p (q t) -> p q t", t=4)
            rows = raw2v[:, :, :, s].rearrange("p t q -> p q t")
            if s in (3,):
                nc.vector.tensor_copy(out=regrouped, in_=rows)
            else:
                nc.scalar.copy(out=regrouped, in_=rows)
        raw2w = raw2[:].bitcast(F32)
        for g in range(2):
            ps2 = psum_ac.tile([P, 512], F32, name="ps2", tag="ac")
            for tt in range(2):
                t = 2 * g + tt
                for u in range(2):
                    nc.tensor.transpose(
                        out=ps2[:, u * 256 + tt * P : u * 256 + (tt + 1) * P],
                        in_=raw2w[:, t * 256 + u : (t + 1) * 256 : 2],
                        identity=ident[:],
                    )
            nc.scalar.copy(
                out=gww[:, g * 512 : (g + 1) * 512].rearrange("p (c u) -> p c u", u=2),
                in_=ps2[:].rearrange("p (u c) -> p c u", u=2),
            )
        nc.scalar.copy(
            out=gww[:, 2048:2560].rearrange("p (c u) -> p c u", u=2),
            in_=ps3[:].rearrange("p (u c) -> p c u", u=2),
        )
        mask_piece_scalar(0)
        mask_piece_scalar(1)
        make_mask(2, 2)
        transposes(2)
        quantise(1, 0, 2)
        quantise_weights(1)
        quantise_weights(0)
        transposes(3)
        first_matmuls(0)
        first_matmuls(1)
        make_up(2)
        make_mask(4, 2)

        for k in range(3, NCH - 2):
            quantise(k - 1, 0, 4 if k - 2 >= L else 2)
            transposes(k + 1)
            first_matmuls(k - 1)
            if k - 2 >= L:
                last_matmuls(k - 2 - L)
            make_up(k)
            if k + 2 in V_MASKS:
                make_mask(k + 2, V_MASKS[k + 2])
            if k == 3:
                quantise_weights(2)
            mask_ac(k - L, pair(k + 1)[:, 2 * H : 4 * H])
            if k in S_STEPS:
                mask_piece_scalar(S_STEPS.index(k) + 2)

        k = NCH - 2
        quantise(k - 1, 0, 4)
        transposes(k + 1)
        first_matmuls(k - 1)
        last_matmuls(k - 2 - L)
        make_up(k)
        make_up(k + 1)
        quantise(k, 0, 4)
        first_matmuls(k)
        last_matmuls(k - 1 - L)
        quantise(k + 1, 0, 2)
        first_matmuls(k + 1)
        lasts = list(range(k - L, NCH))
        filled = {}
        for i, j in enumerate(lasts):
            if i % 2 == 0:
                tile_ac = work.tile([P, 4 * H], BF16, name="pair", tag="pair", bufs=4, align_bytes=64)
            filled[j] = (tile_ac, i % 2)
            mask_ac(j, tile_ac[:, i % 2 * 2 * H : (i % 2 + 1) * 2 * H])
            if i in (2, 3, 4):
                first = lasts[{2: 0, 3: 2, 4: 4}[i]]
                src = filled[first][0]
                width = 4 if i < 4 else 2
                cd = work.tile([P, 4 * P], U32, name="cd", tag="cd", bufs=4, align_bytes=64)
                sc = work.tile([P, 4 * P], U8, name="sc", tag="sc", bufs=4, align_bytes=64)
                nc.vector.quantize_mx(
                    out=cd[:, 0 : width * P].bitcast(FP8X4),
                    scales=sc[:, 0 : width * P],
                    in_=src[:, 0 : width * H],
                )
                for h in range(width // 2):
                    accodes[first + h] = (cd, sc, h)
                    last_matmuls(first + h)
